import numpy as np
import ml_dtypes


def mxq(x, axis, fmt="e4m3"):
    dtype, down = {"e4m3": (ml_dtypes.float8_e4m3fn, 7), "e5m2": (ml_dtypes.float8_e5m2, 14)}[fmt]
    v = np.moveaxis(np.asarray(x, np.float32).astype(ml_dtypes.bfloat16).astype(np.float64), axis, -1)
    blocks = v.reshape(v.shape[:-1] + (-1, 32))
    amax = np.abs(blocks).max(-1, keepdims=True)
    byte = np.maximum(np.where(amax > 0, np.frexp(amax)[1] - 1 + 127, 0) - down, 1)
    scale = np.exp2(byte - 127.0)
    codes = (blocks / scale).astype(np.float32).astype(dtype).astype(np.float64)
    return np.moveaxis((codes * scale).reshape(v.shape), -1, axis)


WIDE = False


def mx_kscale(k):
    if not WIDE:
        return np.ones(k)
    levels = np.array([10, -10, 5, -5, 0])
    if k % 512:
        return np.exp2(np.random.permutation(np.resize(levels, k // 32))).repeat(32)
    a = np.empty((k // 512, 16))
    for p in range(k // 512):
        a[p, :8] = np.random.permutation(np.resize(levels, 8))
        for g in range(8):
            far = levels[np.abs(levels - a[p, g]) >= 10]
            a[p, g + 8] = far[np.random.randint(len(far))]
    return np.exp2(a.ravel()).repeat(32)


BF16 = ml_dtypes.bfloat16


def bf(x):
    return np.asarray(x, np.float32).astype(BF16)


def f64(x):
    return np.asarray(x).astype(np.float64)


B, S, HID, H, HK, D = 4, 2048, 512, 2, 2, 64
EPS = 1e-6
PRE = 0.004


def rmsnorm(v, w):
    var = np.mean(v * v, axis=-1, keepdims=True)
    return w * (v * (1.0 / np.sqrt(var + EPS)))


def rope(v, cos, sin):
    c = cos[:, :, None, :]
    sn = sin[:, :, None, :]
    v1, v2 = np.split(v, 2, axis=-1)
    rot = np.concatenate([-v2, v1], axis=-1)
    return v * c + rot * sn


def setup_inputs():
    s = mx_kscale(HID)
    return {
        "hidden_states": bf(np.random.standard_normal((B, S, HID)) * s),
        "cos": bf(np.cos(np.random.standard_normal((B, S, D)))),
        "sin": bf(np.sin(np.random.standard_normal((B, S, D)))),
        "Wq_query": bf(np.random.standard_normal((H * D, HID)) * PRE / np.sqrt(HID) / s),
        "Wk": bf(np.random.standard_normal((HK * D, HID)) * PRE / np.sqrt(HID) / s),
        "q_norm_w": bf(1.0 + 0.1 * np.random.standard_normal(D)),
        "k_norm_w": bf(1.0 + 0.1 * np.random.standard_normal(D)),
    }


def reference(hidden_states, cos, sin, Wq_query, Wk, q_norm_w, k_norm_w):
    xq = mxq(f64(hidden_states), 2, "e4m3")
    q = (xq @ mxq(f64(Wq_query), 1, "e4m3").T).reshape(B, S, H, D)
    k = (xq @ mxq(f64(Wk), 1, "e4m3").T).reshape(B, S, HK, D)
    q = rmsnorm(q, f64(q_norm_w))
    k = rmsnorm(k, f64(k_norm_w))
    q = rope(q, f64(cos), f64(sin))
    k = rope(k, f64(cos), f64(sin))
    return q, k

@@ -1,0 +1,288 @@
+from contextlib import ExitStack
+
+import concourse.mybir as mybir
+from concourse.masks import make_identity
+
+F32 = mybir.dt.float32
+BF16 = mybir.dt.bfloat16
+U32 = mybir.dt.uint32
+U8 = mybir.dt.uint8
+FP8X4 = mybir.dt.float8_e4m3fn_x4
+ALU = mybir.AluOpType
+ACT = mybir.ActivationFunctionType
+
+P = 128
+HID = 512
+D = 64
+HALF = 32
+NT = 64
+GT = 4
+NG = NT // GT
+CST = 16
+GPC = CST // GT
+EPS = 1e-6
+NIND = 48
+FLOPS = 2 * 8192 * 512 * 256
+
+
+def tile_qwen3nextattentionforengine_pa_t_kernel(
+    tc, hidden_states, cos, sin, Wq_query, Wk, q_norm_w, k_norm_w, out_0, out_1
+):
+    nc = tc.nc
+    x_v = hidden_states.rearrange("b (s c) k -> (b s) c k", c=NT)
+    cos_v = cos.rearrange("b (s c) j -> (b s) c j", c=NT)
+    sin_v = sin.rearrange("b (s c) j -> (b s) c j", c=NT)
+    out_v = [
+        out_0.rearrange("b (s c) h d -> (b s) c (h d)", c=NT),
+        out_1.rearrange("b (s c) h d -> (b s) c (h d)", c=NT),
+    ]
+
+    with ExitStack() as ctx:
+        const = ctx.enter_context(tc.tile_pool(name="const", bufs=1))
+        xp = ctx.enter_context(tc.tile_pool(name="xp", bufs=NG))
+        csp = ctx.enter_context(tc.tile_pool(name="csp", bufs=NT // CST))
+        grp = ctx.enter_context(tc.tile_pool(name="grp", bufs=3))
+        cdp = ctx.enter_context(tc.tile_pool(name="cdp", bufs=3))
+        sqp = ctx.enter_context(tc.tile_pool(name="sqp", bufs=4))
+        stp = ctx.enter_context(tc.tile_pool(name="stp", bufs=4))
+        ttp = ctx.enter_context(tc.tile_pool(name="ttp", bufs=3))
+        outp = ctx.enter_context(tc.tile_pool(name="outp", bufs=4))
+        ps_t = ctx.enter_context(tc.psum_pool(name="ps_t", bufs=2))
+        ps_v = ctx.enter_context(tc.psum_pool(name="ps_v", bufs=2))
+        ps_u = ctx.enter_context(tc.psum_pool(name="ps_u", bufs=3))
+        ps_s = ctx.enter_context(tc.psum_pool(name="ps_s", bufs=1))
+        ctx.enter_context(tc.manual_schedule())
+
+        eps_t = const.tile([P, 1], F32)
+        nc.vector.memset(eps_t[:], EPS)
+        ident = const.tile([P, P], F32)
+        make_identity(nc, ident[:])
+        ident_b = const.tile([P, P], BF16)
+        make_identity(nc, ident_b[:])
+        zrow = const.tile([P, P], BF16)
+        nc.vector.memset(zrow[:], 0.0)
+        ind = const.tile([P, NIND], F32)
+        nc.vector.memset(ind[:], 0.0)
+        nc.vector.memset(ind[0:D, 0:1], 1.0 / D)
+        nc.vector.memset(ind[D:P, 1:2], 1.0 / D)
+
+        w_sb = const.tile([P, 2 * HID], BF16)
+        nc.scalar.dma_start(out=w_sb[:, 0:HID], in_=Wq_query)
+        nc.scalar.dma_start(out=w_sb[:, HID : 2 * HID], in_=Wk)
+        for y, gain in enumerate((q_norm_w, k_norm_w)):
+            row = gain.rearrange("(o d) -> o d", o=1)
+            nc.scalar.dma_start(out=zrow[y : y + 1, 0:D], in_=row)
+            nc.scalar.dma_start(out=zrow[y : y + 1, D:P], in_=row)
+        warm = const.tile([P, 1], F32)
+        nc.scalar.activation(out=warm[:], in_=eps_t[:], func=ACT.Sqrt)
+
+        x_sb = []
+        cs_sb = []
+        sraw_sb = []
+        for g in range(NG):
+            xg = xp.tile([P, GT * HID], BF16, name="xg")
+            nc.sync.dma_start(
+                out=xg[:].rearrange("p (c k) -> p c k", c=GT), in_=x_v[:, g * GT : (g + 1) * GT, :]
+            )
+            x_sb.append(xg)
+            if g % GPC == 0:
+                c0 = g * GT
+                cs = csp.tile([P, 2 * CST * D], BF16, name="cs")
+                nc.sync.dma_start(
+                    out=cs[:, 0 : CST * D].rearrange("p (c j) -> p c j", c=CST),
+                    in_=cos_v[:, c0 : c0 + CST, :],
+                )
+                sraw = csp.tile([P, CST * D], BF16, name="sraw")
+                nc.sync.dma_start(
+                    out=sraw[:].rearrange("p (c j) -> p c j", c=CST), in_=sin_v[:, c0 : c0 + CST, :]
+                )
+                cs_sb.append(cs)
+                sraw_sb.append(sraw)
+
+        w_f = w_sb[:].bitcast(F32)
+        wt = ps_t.tile([P, 512], F32, name="xt")
+        for i in range(4):
+            y, u = i // 2, i % 2
+            nc.tensor.transpose(
+                wt[:, i * P : (i + 1) * P], w_f[:, y * 256 + u : (y + 1) * 256 : 2], ident[:]
+            )
+        w_gr = const.tile([P, 1024], BF16, align_bytes=64)
+        nc.vector.tensor_copy(
+            out=w_gr[:].bitcast(F32).rearrange("p (t f u) -> p t f u", t=2, u=2),
+            in_=wt[:].rearrange("p (t u f) -> p t f u", t=2, u=2),
+        )
+        w_codes = const.tile([P, 256], U32, align_bytes=64)
+        w_scales = const.tile([P, 256], U8, align_bytes=64)
+        nc.vector.quantize_mx(out=w_codes[:].bitcast(FP8X4), scales=w_scales[:], in_=w_gr[:])
+
+        gt_ps = ps_t.tile([P, P], BF16, name="xt")
+        nc.tensor.transpose(gt_ps[:], zrow[:], ident_b[:])
+        wcol = const.tile([P, 2], F32)
+        nc.vector.tensor_copy(out=wcol[:], in_=gt_ps[:, 0:2])
+
+        st = {}
+
+        def stage_cs(k):
+            dst = cs_sb[k][:, CST * D : 2 * CST * D].rearrange("p (c j) -> p c j", c=CST)
+            src = sraw_sb[k][:].rearrange("p (c j) -> p c j", c=CST)
+            nc.gpsimd.tensor_scalar(
+                out=dst[:, :, 0:HALF], in0=src[:, :, HALF:D], scalar1=1.0, scalar2=0.0,
+                op0=ALU.mult, op1=ALU.add,
+            )
+            nc.gpsimd.tensor_scalar(
+                out=dst[:, :, HALF:D], in0=src[:, :, 0:HALF], scalar1=-1.0, scalar2=0.0,
+                op0=ALU.mult, op1=ALU.add,
+            )
+
+        def stage_a(g):
+            x_f = x_sb[g][:].bitcast(F32)
+            for h in range(2):
+                xt = ps_t.tile([P, 512], F32, name="xt")
+                for i in range(4):
+                    t, u = h * 2 + i // 2, i % 2
+                    nc.tensor.transpose(
+                        xt[:, i * P : (i + 1) * P], x_f[:, t * 256 + u : (t + 1) * 256 : 2], ident[:]
+                    )
+                st[("xt", g, h)] = xt
+
+        def stage_b(g):
+            gr = grp.tile([P, GT * 512], BF16, name="gr", align_bytes=64)
+            gr_f = gr[:].bitcast(F32)
+            for h in range(2):
+                nc.scalar.copy(
+                    out=gr_f[:, h * 512 : (h + 1) * 512].rearrange("p (t r u) -> p t r u", t=2, u=2),
+                    in_=st[("xt", g, h)][:].rearrange("p (t u r) -> p t r u", t=2, u=2),
+                )
+            st[("gr", g)] = gr
+
+        def stage_c(g):
+            codes = cdp.tile([P, GT * P], U32, name="codes", align_bytes=64)
+            scales = cdp.tile([P, GT * P], U8, name="scales", align_bytes=64)
+            nc.vector.quantize_mx(out=codes[:].bitcast(FP8X4), scales=scales[:], in_=st[("gr", g)][:])
+            st[("cd", g)] = (codes, scales)
+
+        def stage_d(g):
+            codes, scales = st[("cd", g)]
+            for y in range(2):
+                vt = ps_v.tile([P, 512], F32, name="vt")
+                nc.tensor.matmul_mx(
+                    out=vt[:],
+                    lhsT=w_codes[:, y * P : (y + 1) * P].bitcast(FP8X4),
+                    lhsT_scale=w_scales[:, y * P : (y + 1) * P],
+                    rhs=codes[:].bitcast(FP8X4),
+                    rhs_scale=scales[:],
+                    start=True,
+                    stop=True,
+                )
+                st[("vt", g, y)] = vt
+
+        def stage_e(g):
+            for y in range(2):
+                vt = st[("vt", g, y)]
+                sq = sqp.tile([P, 512], F32, name="sq")
+                nc.scalar.activation(out=sq[:], in_=vt[:], func=ACT.Square)
+                ut = sqp.tile([P, 512], F32, name="ut")
+                nc.scalar.activation(out=ut[:], in_=vt[:], func=ACT.Copy, scale=wcol[:, y : y + 1])
+                st[("sq", g, y)] = sq
+                st[("ut", g, y)] = ut
+
+        def stage_mt(g):
+            ssp = ps_s.tile([P, 2 * GT * NIND], F32, name="ssp")
+            ups = [ps_u.tile([P, 512], F32, name="up") for hb in range(2)]
+            for q in range(4):
+                for m in (2 * q, 2 * q + 1):
+                    y = m // GT
+                    t = m % GT
+                    k = t * 2 + y
+                    nc.tensor.matmul(
+                        out=ssp[:, k * NIND : (k + 1) * NIND],
+                        lhsT=st[("sq", g, y)][:, t * P : (t + 1) * P],
+                        rhs=ind[:],
+                        start=True,
+                        stop=True,
+                    )
+                for y in range(2):
+                    c = (q % 2) * 256 + y * P
+                    nc.tensor.transpose(
+                        ups[q // 2][:, c : c + P], st[("ut", g, y)][:, q * P : (q + 1) * P], ident[:]
+                    )
+            st[("ssp", g)] = ssp
+            st[("up", g, 0)] = ups[0]
+            st[("up", g, 1)] = ups[1]
+
+        def stage_r(g):
+            std = stp.tile([P, GT * 4], F32, name="std")
+            nc.scalar.activation(
+                out=std[:].rearrange("p (k n) -> p k n", n=2),
+                in_=st[("ssp", g)][:].rearrange("p (k n) -> p k n", n=NIND)[:, :, 0:2],
+                func=ACT.Sqrt,
+                bias=eps_t[:, 0:1],
+            )
+            st[("std", g)] = std
+
+        def stage_f(g):
+            rstd = stp.tile([P, GT * 4], F32, name="rstd")
+            nc.vector.reciprocal(out=rstd[:], in_=st[("std", g)][:])
+            tt = ttp.tile([P, GT * 4 * 2 * D], F32, name="tt")
+            csv = cs_sb[g // GPC][:].rearrange("p (r c j) -> p r c j", r=2, c=CST)
+            for hb in range(2):
+                up = st[("up", g, hb)]
+                for t2 in range(2):
+                    t = hb * 2 + t2
+                    for yh in range(4):
+                        si = t * 4 + yh
+                        ti = (yh // 2) * 8 + t * 2 + yh % 2
+                        c = t2 * 256 + yh * D
+                        nc.vector.scalar_tensor_tensor(
+                            out=tt[:, ti * 128 : (ti + 1) * 128].rearrange("p (r j) -> p r j", r=2),
+                            in0=up[:, c : c + D].unsqueeze(1).to_broadcast([P, 2, D]),
+                            scalar=rstd[:, si : si + 1],
+                            in1=csv[:, :, (g % GPC) * GT + t, :],
+                            op0=ALU.mult,
+                            op1=ALU.mult,
+                        )
+            st[("tt", g)] = tt
+
+        def stage_h(g):
+            ttv = st[("tt", g)][:].rearrange("p (n r j) -> p n r j", r=2, j=D)
+            o = outp.tile([P, 2 * GT * 128], F32, name="o")
+            ov = o[:].rearrange("p (n j) -> p n j", j=D)
+            for half in range(2):
+                a = half * HALF
+                b = (1 - half) * HALF
+                nc.gpsimd.tensor_tensor(
+                    out=ov[:, :, a : a + HALF],
+                    in0=ttv[:, :, 0, a : a + HALF],
+                    in1=ttv[:, :, 1, b : b + HALF],
+                    op=ALU.add,
+                )
+            for y in range(2):
+                nc.sync.dma_start(
+                    out=out_v[y][:, g * GT : (g + 1) * GT, :],
+                    in_=o[:, y * GT * 128 : (y + 1) * GT * 128].rearrange("p (t f) -> p t f", t=GT),
+                )
+
+        def on(g):
+            return 0 <= g < NG
+
+        for i in range(NG + 5):
+            if i % GPC == 0 and i < NG:
+                stage_cs(i // GPC)
+            if on(i):
+                stage_a(i)
+            if on(i - 2):
+                stage_c(i - 2)
+            if on(i - 1):
+                stage_b(i - 1)
+            if on(i - 2):
+                stage_d(i - 2)
+            if on(i - 3):
+                stage_e(i - 3)
+            if on(i - 5):
+                stage_f(i - 5)
+            if on(i - 4):
+                stage_r(i - 4)
+            if on(i - 3):
+                stage_mt(i - 3)
+            if on(i - 5):
+                stage_h(i - 5)

@@ -16,12 +16,12 @@ HID = 512
 D = 64
 HALF = 32
 NT = 64
-GT = 4
-NG = NT // GT
+UNITS = [1, 1] + [2] * 30 + [1, 1]
+XLOADS = [1, 1, 2] + [4] * 15
 CST = 16
-GPC = CST // GT
+SWT = 4
+AHEAD = 24
 EPS = 1e-6
-NIND = 48
 FLOPS = 2 * 8192 * 512 * 256
 
 
@@ -36,71 +36,88 @@ def tile_qwen3nextattentionforengine_pa_t_kernel(
         out_0.rearrange("b (s c) h d -> (b s) c (h d)", c=NT),
         out_1.rearrange("b (s c) h d -> (b s) c (h d)", c=NT),
     ]
+    first = [sum(UNITS[:k]) for k in range(len(UNITS))]
+    NU = len(UNITS)
 
     with ExitStack() as ctx:
         const = ctx.enter_context(tc.tile_pool(name="const", bufs=1))
-        xp = ctx.enter_context(tc.tile_pool(name="xp", bufs=NG))
+        xp = ctx.enter_context(tc.tile_pool(name="xp", bufs=1))
         csp = ctx.enter_context(tc.tile_pool(name="csp", bufs=NT // CST))
-        grp = ctx.enter_context(tc.tile_pool(name="grp", bufs=3))
-        cdp = ctx.enter_context(tc.tile_pool(name="cdp", bufs=3))
-        sqp = ctx.enter_context(tc.tile_pool(name="sqp", bufs=4))
+        grp = ctx.enter_context(tc.tile_pool(name="grp", bufs=4))
+        cdp = ctx.enter_context(tc.tile_pool(name="cdp", bufs=4))
+        utp = ctx.enter_context(tc.tile_pool(name="utp", bufs=4))
+        jkp = ctx.enter_context(tc.tile_pool(name="jkp", bufs=4))
         stp = ctx.enter_context(tc.tile_pool(name="stp", bufs=4))
-        ttp = ctx.enter_context(tc.tile_pool(name="ttp", bufs=3))
-        outp = ctx.enter_context(tc.tile_pool(name="outp", bufs=4))
-        ps_t = ctx.enter_context(tc.psum_pool(name="ps_t", bufs=2))
+        ttp = ctx.enter_context(tc.tile_pool(name="ttp", bufs=4))
+        outp = ctx.enter_context(tc.tile_pool(name="outp", bufs=6))
+        ps_x = ctx.enter_context(tc.psum_pool(name="ps_x", bufs=2))
         ps_v = ctx.enter_context(tc.psum_pool(name="ps_v", bufs=2))
-        ps_u = ctx.enter_context(tc.psum_pool(name="ps_u", bufs=3))
-        ps_s = ctx.enter_context(tc.psum_pool(name="ps_s", bufs=1))
+        ps_a = ctx.enter_context(tc.psum_pool(name="ps_a", bufs=2))
+        ps_u = ctx.enter_context(tc.psum_pool(name="ps_u", bufs=2))
         ctx.enter_context(tc.manual_schedule())
-
-        eps_t = const.tile([P, 1], F32)
-        nc.vector.memset(eps_t[:], EPS)
-        ident = const.tile([P, P], F32)
-        make_identity(nc, ident[:])
-        ident_b = const.tile([P, P], BF16)
-        make_identity(nc, ident_b[:])
-        zrow = const.tile([P, P], BF16)
-        nc.vector.memset(zrow[:], 0.0)
-        ind = const.tile([P, NIND], F32)
-        nc.vector.memset(ind[:], 0.0)
-        nc.vector.memset(ind[0:D, 0:1], 1.0 / D)
-        nc.vector.memset(ind[D:P, 1:2], 1.0 / D)
 
         w_sb = const.tile([P, 2 * HID], BF16)
         nc.scalar.dma_start(out=w_sb[:, 0:HID], in_=Wq_query)
         nc.scalar.dma_start(out=w_sb[:, HID : 2 * HID], in_=Wk)
+
+        x_tile = {}
+        cs_sb = {}
+        sraw_sb = {}
+
+        def load_cs(j):
+            c0 = j * CST
+            cs = csp.tile([P, 2 * CST * D], BF16, name="cs")
+            nc.sync.dma_start(
+                out=cs[:, 0 : CST * D].rearrange("p (c j) -> p c j", c=CST),
+                in_=cos_v[:, c0 : c0 + CST, :],
+            )
+            sraw = csp.tile([P, CST * D], BF16, name="sraw")
+            nc.sync.dma_start(
+                out=sraw[:].rearrange("p (c j) -> p c j", c=CST), in_=sin_v[:, c0 : c0 + CST, :]
+            )
+            cs_sb[j] = cs
+            sraw_sb[j] = sraw
+
+        def load_x(l):
+            c0 = sum(XLOADS[:l])
+            n = XLOADS[l]
+            xg = xp.tile([P, n * HID], BF16, name="x%d" % l)
+            nc.sync.dma_start(
+                out=xg[:].rearrange("p (c k) -> p c k", c=n), in_=x_v[:, c0 : c0 + n, :]
+            )
+            for t in range(n):
+                x_tile[c0 + t] = (xg, t)
+            if l == 3:
+                load_cs(0)
+            elif l > 3 and c0 % CST == 0:
+                load_cs(c0 // CST)
+
+        loaded = [0]
+
+        def load_until(tile):
+            while loaded[0] < len(XLOADS) and sum(XLOADS[: loaded[0]]) < tile:
+                load_x(loaded[0])
+                loaded[0] += 1
+
+        load_until(AHEAD)
+
+        ident = const.tile([P, P], F32)
+        make_identity(nc, ident[:])
+        ident_b = const.tile([P, P], BF16)
+        make_identity(nc, ident_b[:])
+        eps_t = const.tile([P, 1], F32)
+        nc.vector.memset(eps_t[:], EPS)
+        zrow = const.tile([P, P], BF16)
+        nc.vector.memset(zrow[:], 0.0)
         for y, gain in enumerate((q_norm_w, k_norm_w)):
             row = gain.rearrange("(o d) -> o d", o=1)
             nc.scalar.dma_start(out=zrow[y : y + 1, 0:D], in_=row)
             nc.scalar.dma_start(out=zrow[y : y + 1, D:P], in_=row)
         warm = const.tile([P, 1], F32)
-        nc.scalar.activation(out=warm[:], in_=eps_t[:], func=ACT.Sqrt)
-
-        x_sb = []
-        cs_sb = []
-        sraw_sb = []
-        for g in range(NG):
-            xg = xp.tile([P, GT * HID], BF16, name="xg")
-            nc.sync.dma_start(
-                out=xg[:].rearrange("p (c k) -> p c k", c=GT), in_=x_v[:, g * GT : (g + 1) * GT, :]
-            )
-            x_sb.append(xg)
-            if g % GPC == 0:
-                c0 = g * GT
-                cs = csp.tile([P, 2 * CST * D], BF16, name="cs")
-                nc.sync.dma_start(
-                    out=cs[:, 0 : CST * D].rearrange("p (c j) -> p c j", c=CST),
-                    in_=cos_v[:, c0 : c0 + CST, :],
-                )
-                sraw = csp.tile([P, CST * D], BF16, name="sraw")
-                nc.sync.dma_start(
-                    out=sraw[:].rearrange("p (c j) -> p c j", c=CST), in_=sin_v[:, c0 : c0 + CST, :]
-                )
-                cs_sb.append(cs)
-                sraw_sb.append(sraw)
+        nc.scalar.activation(out=warm[:], in_=eps_t[:], func=ACT.Abs_reciprocal_sqrt)
 
         w_f = w_sb[:].bitcast(F32)
-        wt = ps_t.tile([P, 512], F32, name="xt")
+        wt = ps_v.tile([P, 512], F32, name="vt")
         for i in range(4):
             y, u = i // 2, i % 2
             nc.tensor.transpose(
@@ -115,16 +132,18 @@ def tile_qwen3nextattentionforengine_pa_t_kernel(
         w_scales = const.tile([P, 256], U8, align_bytes=64)
         nc.vector.quantize_mx(out=w_codes[:].bitcast(FP8X4), scales=w_scales[:], in_=w_gr[:])
 
-        gt_ps = ps_t.tile([P, P], BF16, name="xt")
+        gt_ps = ps_u.tile([P, P], BF16, name="up")
         nc.tensor.transpose(gt_ps[:], zrow[:], ident_b[:])
         wcol = const.tile([P, 2], F32)
         nc.vector.tensor_copy(out=wcol[:], in_=gt_ps[:, 0:2])
 
         st = {}
 
-        def stage_cs(k):
-            dst = cs_sb[k][:, CST * D : 2 * CST * D].rearrange("p (c j) -> p c j", c=CST)
-            src = sraw_sb[k][:].rearrange("p (c j) -> p c j", c=CST)
+        def stage_cs(j):
+            c0 = j * SWT % CST
+            dst = cs_sb[j * SWT // CST][:, CST * D : 2 * CST * D].rearrange("p (c j) -> p c j", c=CST)
+            dst = dst[:, c0 : c0 + SWT, :]
+            src = sraw_sb[j * SWT // CST][:].rearrange("p (c j) -> p c j", c=CST)[:, c0 : c0 + SWT, :]
             nc.gpsimd.tensor_scalar(
                 out=dst[:, :, 0:HALF], in0=src[:, :, HALF:D], scalar1=1.0, scalar2=0.0,
                 op0=ALU.mult, op1=ALU.add,
@@ -134,39 +153,43 @@ def tile_qwen3nextattentionforengine_pa_t_kernel(
                 op0=ALU.mult, op1=ALU.add,
             )
 
-        def stage_a(g):
-            x_f = x_sb[g][:].bitcast(F32)
-            for h in range(2):
-                xt = ps_t.tile([P, 512], F32, name="xt")
-                for i in range(4):
-                    t, u = h * 2 + i // 2, i % 2
+        def stage_a(k):
+            xt = ps_x.tile([P, 512], F32, name="xt")
+            for i in range(UNITS[k]):
+                xg, t = x_tile[first[k] + i]
+                x_f = xg[:].bitcast(F32)
+                for u in range(2):
+                    c = (i * 2 + u) * P
                     nc.tensor.transpose(
-                        xt[:, i * P : (i + 1) * P], x_f[:, t * 256 + u : (t + 1) * 256 : 2], ident[:]
+                        xt[:, c : c + P], x_f[:, t * 256 + u : (t + 1) * 256 : 2], ident[:]
                     )
-                st[("xt", g, h)] = xt
+            st[("xt", k)] = xt
 
-        def stage_b(g):
-            gr = grp.tile([P, GT * 512], BF16, name="gr", align_bytes=64)
-            gr_f = gr[:].bitcast(F32)
-            for h in range(2):
-                nc.scalar.copy(
-                    out=gr_f[:, h * 512 : (h + 1) * 512].rearrange("p (t r u) -> p t r u", t=2, u=2),
-                    in_=st[("xt", g, h)][:].rearrange("p (t u r) -> p t r u", t=2, u=2),
-                )
-            st[("gr", g)] = gr
+        def stage_b(k):
+            n = UNITS[k]
+            gr = grp.tile([P, n * 512], BF16, name="gr", align_bytes=64)
+            out = gr[:].bitcast(F32).rearrange("p (t r u) -> p t r u", t=n, u=2)
+            src = st[("xt", k)][:, 0 : n * 256].rearrange("p (t u r) -> p t r u", t=n, u=2)
+            if k % 2 == 0:
+                nc.scalar.copy(out=out, in_=src)
+            else:
+                nc.vector.tensor_copy(out=out, in_=src)
+            st[("gr", k)] = gr
 
-        def stage_c(g):
-            codes = cdp.tile([P, GT * P], U32, name="codes", align_bytes=64)
-            scales = cdp.tile([P, GT * P], U8, name="scales", align_bytes=64)
-            nc.vector.quantize_mx(out=codes[:].bitcast(FP8X4), scales=scales[:], in_=st[("gr", g)][:])
-            st[("cd", g)] = (codes, scales)
+        def stage_c(k):
+            n = UNITS[k]
+            codes = cdp.tile([P, n * P], U32, name="codes", align_bytes=64)
+            scales = cdp.tile([P, n * P], U8, name="scales", align_bytes=64)
+            nc.vector.quantize_mx(out=codes[:].bitcast(FP8X4), scales=scales[:], in_=st[("gr", k)][:])
+            st[("cd", k)] = (codes, scales)
 
-        def stage_d(g):
-            codes, scales = st[("cd", g)]
+        def stage_d(k):
+            n = UNITS[k]
+            codes, scales = st[("cd", k)]
+            vt = ps_v.tile([P, 512], F32, name="vt")
             for y in range(2):
-                vt = ps_v.tile([P, 512], F32, name="vt")
                 nc.tensor.matmul_mx(
-                    out=vt[:],
+                    out=vt[:, y * n * P : (y + 1) * n * P],
                     lhsT=w_codes[:, y * P : (y + 1) * P].bitcast(FP8X4),
                     lhsT_scale=w_scales[:, y * P : (y + 1) * P],
                     rhs=codes[:].bitcast(FP8X4),
@@ -174,78 +197,86 @@ def tile_qwen3nextattentionforengine_pa_t_kernel(
                     start=True,
                     stop=True,
                 )
-                st[("vt", g, y)] = vt
+            va = ps_a.tile([P, 512], F32, name="va")
+            for t in range(n):
+                nc.tensor.matmul_mx(
+                    out=va[:, t * 256 : (t + 1) * 256],
+                    lhsT=codes[:, t * P : (t + 1) * P].bitcast(FP8X4),
+                    lhsT_scale=scales[:, t * P : (t + 1) * P],
+                    rhs=w_codes[:].bitcast(FP8X4),
+                    rhs_scale=w_scales[:],
+                    start=True,
+                    stop=True,
+                )
+            st[("vt", k)] = vt
+            st[("va", k)] = va
 
-        def stage_e(g):
+        def stage_u(k):
+            n = UNITS[k]
+            ut = utp.tile([P, n * 256], F32, name="ut")
             for y in range(2):
-                vt = st[("vt", g, y)]
-                sq = sqp.tile([P, 512], F32, name="sq")
-                nc.scalar.activation(out=sq[:], in_=vt[:], func=ACT.Square)
-                ut = sqp.tile([P, 512], F32, name="ut")
-                nc.scalar.activation(out=ut[:], in_=vt[:], func=ACT.Copy, scale=wcol[:, y : y + 1])
-                st[("sq", g, y)] = sq
-                st[("ut", g, y)] = ut
+                nc.scalar.activation(
+                    out=ut[:, y * n * P : (y + 1) * n * P],
+                    in_=st[("vt", k)][:, y * n * P : (y + 1) * n * P],
+                    func=ACT.Copy,
+                    scale=wcol[:, y : y + 1],
+                )
+            st[("ut", k)] = ut
 
-        def stage_mt(g):
-            ssp = ps_s.tile([P, 2 * GT * NIND], F32, name="ssp")
-            ups = [ps_u.tile([P, 512], F32, name="up") for hb in range(2)]
-            for q in range(4):
-                for m in (2 * q, 2 * q + 1):
-                    y = m // GT
-                    t = m % GT
-                    k = t * 2 + y
-                    nc.tensor.matmul(
-                        out=ssp[:, k * NIND : (k + 1) * NIND],
-                        lhsT=st[("sq", g, y)][:, t * P : (t + 1) * P],
-                        rhs=ind[:],
-                        start=True,
-                        stop=True,
-                    )
-                for y in range(2):
-                    c = (q % 2) * 256 + y * P
-                    nc.tensor.transpose(
-                        ups[q // 2][:, c : c + P], st[("ut", g, y)][:, q * P : (q + 1) * P], ident[:]
-                    )
-            st[("ssp", g)] = ssp
-            st[("up", g, 0)] = ups[0]
-            st[("up", g, 1)] = ups[1]
-
-        def stage_r(g):
-            std = stp.tile([P, GT * 4], F32, name="std")
+        def stage_q(k):
+            n = UNITS[k]
+            va = st[("va", k)]
+            junk = jkp.tile([P, n * 256], BF16, name="junk")
+            ss = stp.tile([P, n * 4], F32, name="ss")
+            for i in range(n * 4):
+                nc.scalar.activation(
+                    out=junk[:, i * D : (i + 1) * D],
+                    in_=va[:, i * D : (i + 1) * D],
+                    func=ACT.Square,
+                    accum_out=ss[:, i : i + 1],
+                )
+            rstd = stp.tile([P, n * 4], F32, name="rstd")
             nc.scalar.activation(
-                out=std[:].rearrange("p (k n) -> p k n", n=2),
-                in_=st[("ssp", g)][:].rearrange("p (k n) -> p k n", n=NIND)[:, :, 0:2],
-                func=ACT.Sqrt,
-                bias=eps_t[:, 0:1],
+                out=rstd[:], in_=ss[:], func=ACT.Abs_reciprocal_sqrt, scale=1.0 / D, bias=eps_t[:, 0:1]
             )
-            st[("std", g)] = std
+            st[("rstd", k)] = rstd
 
-        def stage_f(g):
-            rstd = stp.tile([P, GT * 4], F32, name="rstd")
-            nc.vector.reciprocal(out=rstd[:], in_=st[("std", g)][:])
-            tt = ttp.tile([P, GT * 4 * 2 * D], F32, name="tt")
-            csv = cs_sb[g // GPC][:].rearrange("p (r c j) -> p r c j", r=2, c=CST)
-            for hb in range(2):
-                up = st[("up", g, hb)]
-                for t2 in range(2):
-                    t = hb * 2 + t2
-                    for yh in range(4):
-                        si = t * 4 + yh
-                        ti = (yh // 2) * 8 + t * 2 + yh % 2
-                        c = t2 * 256 + yh * D
-                        nc.vector.scalar_tensor_tensor(
-                            out=tt[:, ti * 128 : (ti + 1) * 128].rearrange("p (r j) -> p r j", r=2),
-                            in0=up[:, c : c + D].unsqueeze(1).to_broadcast([P, 2, D]),
-                            scalar=rstd[:, si : si + 1],
-                            in1=csv[:, :, (g % GPC) * GT + t, :],
-                            op0=ALU.mult,
-                            op1=ALU.mult,
-                        )
-            st[("tt", g)] = tt
+        def stage_t(k):
+            n = UNITS[k]
+            up = ps_u.tile([P, 512], F32, name="up")
+            ut = st[("ut", k)]
+            for t in range(n):
+                for y in range(2):
+                    c = (t * 2 + y) * P
+                    s = (y * n + t) * P
+                    nc.tensor.transpose(up[:, c : c + P], ut[:, s : s + P], ident[:])
+            st[("up", k)] = up
 
-        def stage_h(g):
-            ttv = st[("tt", g)][:].rearrange("p (n r j) -> p n r j", r=2, j=D)
-            o = outp.tile([P, 2 * GT * 128], F32, name="o")
+        def stage_f(k):
+            n = UNITS[k]
+            rstd = st[("rstd", k)]
+            up = st[("up", k)]
+            tt = ttp.tile([P, n * 512], F32, name="tt")
+            for t in range(n):
+                tile = first[k] + t
+                csv = cs_sb[tile // CST][:].rearrange("p (r c j) -> p r c j", r=2, c=CST)
+                for yh in range(4):
+                    si = t * 4 + yh
+                    ti = (yh // 2) * 2 * n + t * 2 + yh % 2
+                    nc.vector.scalar_tensor_tensor(
+                        out=tt[:, ti * 128 : (ti + 1) * 128].rearrange("p (r j) -> p r j", r=2),
+                        in0=up[:, si * D : (si + 1) * D].unsqueeze(1).to_broadcast([P, 2, D]),
+                        scalar=rstd[:, si : si + 1],
+                        in1=csv[:, :, tile % CST, :],
+                        op0=ALU.mult,
+                        op1=ALU.mult,
+                    )
+            st[("tt", k)] = tt
+
+        def stage_h(k):
+            n = UNITS[k]
+            ttv = st[("tt", k)][:].rearrange("p (n r j) -> p n r j", r=2, j=D)
+            o = outp.tile([P, n * 256], F32, name="o")
             ov = o[:].rearrange("p (n j) -> p n j", j=D)
             for half in range(2):
                 a = half * HALF
@@ -258,31 +289,30 @@ def tile_qwen3nextattentionforengine_pa_t_kernel(
                 )
             for y in range(2):
                 nc.sync.dma_start(
-                    out=out_v[y][:, g * GT : (g + 1) * GT, :],
-                    in_=o[:, y * GT * 128 : (y + 1) * GT * 128].rearrange("p (t f) -> p t f", t=GT),
+                    out=out_v[y][:, first[k] : first[k] + n, :],
+                    in_=o[:, y * n * 128 : (y + 1) * n * 128].rearrange("p (t f) -> p t f", t=n),
                 )
 
-        def on(g):
-            return 0 <= g < NG
+        def on(k):
+            return 0 <= k < NU
 
-        for i in range(NG + 5):
-            if i % GPC == 0 and i < NG:
-                stage_cs(i // GPC)
+        for i in range(NU + 5):
             if on(i):
-                stage_a(i)
+                load_until(first[i] + AHEAD)
+            if on(i - 3):
+                stage_d(i - 3)
+            if on(i - 4):
+                stage_u(i - 4)
+                stage_t(i - 4)
+                stage_q(i - 4)
             if on(i - 2):
                 stage_c(i - 2)
             if on(i - 1):
                 stage_b(i - 1)
-            if on(i - 2):
-                stage_d(i - 2)
-            if on(i - 3):
-                stage_e(i - 3)
+            if on(i):
+                stage_a(i)
             if on(i - 5):
                 stage_f(i - 5)
-            if on(i - 4):
-                stage_r(i - 4)
-            if on(i - 3):
-                stage_mt(i - 3)
-            if on(i - 5):
                 stage_h(i - 5)
+            if on(i - 3) and first[i - 3] % SWT == 0:
+                stage_cs(first[i - 3] // SWT)

@@ -265,9 +265,9 @@ def tile_qwen3nextattentionforengine_pa_t_kernel(
                     ti = (yh // 2) * 2 * n + t * 2 + yh % 2
                     nc.vector.scalar_tensor_tensor(
                         out=tt[:, ti * 128 : (ti + 1) * 128].rearrange("p (r j) -> p r j", r=2),
-                        in0=up[:, si * D : (si + 1) * D].unsqueeze(1).to_broadcast([P, 2, D]),
+                        in0=csv[:, :, tile % CST, :],
                         scalar=rstd[:, si : si + 1],
-                        in1=csv[:, :, tile % CST, :],
+                        in1=up[:, si * D : (si + 1) * D].unsqueeze(1).to_broadcast([P, 2, D]),
                         op0=ALU.mult,
                         op1=ALU.mult,
                     )

@@ -170,10 +170,7 @@ def tile_qwen3nextattentionforengine_pa_t_kernel(
             gr = grp.tile([P, n * 512], BF16, name="gr", align_bytes=64)
             out = gr[:].bitcast(F32).rearrange("p (t r u) -> p t r u", t=n, u=2)
             src = st[("xt", k)][:, 0 : n * 256].rearrange("p (t u r) -> p t r u", t=n, u=2)
-            if k % 2 == 0:
-                nc.scalar.copy(out=out, in_=src)
-            else:
-                nc.vector.tensor_copy(out=out, in_=src)
+            nc.scalar.copy(out=out, in_=src)
             st[("gr", k)] = gr
 
         def stage_c(k):
@@ -278,15 +275,12 @@ def tile_qwen3nextattentionforengine_pa_t_kernel(
             ttv = st[("tt", k)][:].rearrange("p (n r j) -> p n r j", r=2, j=D)
             o = outp.tile([P, n * 256], F32, name="o")
             ov = o[:].rearrange("p (n j) -> p n j", j=D)
-            for half in range(2):
-                a = half * HALF
-                b = (1 - half) * HALF
-                nc.gpsimd.tensor_tensor(
-                    out=ov[:, :, a : a + HALF],
-                    in0=ttv[:, :, 0, a : a + HALF],
-                    in1=ttv[:, :, 1, b : b + HALF],
-                    op=ALU.add,
-                )
+            nc.gpsimd.tensor_tensor(
+                out=ov.rearrange("p n (a i) -> p n a i", a=2),
+                in0=ttv[:, :, 0, :].rearrange("p n (a i) -> p n a i", a=2),
+                in1=ttv[:, :, 1, :].rearrange("p n (a i) -> p n a i", a=2)[:, :, ::-1, :],
+                op=ALU.add,
+            )
             for y in range(2):
                 nc.sync.dma_start(
                     out=out_v[y][:, first[k] : first[k] + n, :],

@@ -22,6 +22,7 @@ CST = 16
 SWT = 4
 AHEAD = 24
 EPS = 1e-6
+NIND = 48
 FLOPS = 2 * 8192 * 512 * 256
 
 
@@ -46,13 +47,13 @@ def tile_qwen3nextattentionforengine_pa_t_kernel(
         grp = ctx.enter_context(tc.tile_pool(name="grp", bufs=4))
         cdp = ctx.enter_context(tc.tile_pool(name="cdp", bufs=4))
         utp = ctx.enter_context(tc.tile_pool(name="utp", bufs=4))
-        jkp = ctx.enter_context(tc.tile_pool(name="jkp", bufs=4))
+        sqp = ctx.enter_context(tc.tile_pool(name="sqp", bufs=4))
         stp = ctx.enter_context(tc.tile_pool(name="stp", bufs=4))
         ttp = ctx.enter_context(tc.tile_pool(name="ttp", bufs=4))
         outp = ctx.enter_context(tc.tile_pool(name="outp", bufs=6))
         ps_x = ctx.enter_context(tc.psum_pool(name="ps_x", bufs=2))
         ps_v = ctx.enter_context(tc.psum_pool(name="ps_v", bufs=2))
-        ps_a = ctx.enter_context(tc.psum_pool(name="ps_a", bufs=2))
+        ps_s = ctx.enter_context(tc.psum_pool(name="ps_s", bufs=2))
         ps_u = ctx.enter_context(tc.psum_pool(name="ps_u", bufs=2))
         ctx.enter_context(tc.manual_schedule())
 
@@ -109,6 +110,10 @@ def tile_qwen3nextattentionforengine_pa_t_kernel(
         nc.vector.memset(eps_t[:], EPS)
         zrow = const.tile([P, P], BF16)
         nc.vector.memset(zrow[:], 0.0)
+        ind = const.tile([P, NIND], F32)
+        nc.vector.memset(ind[:], 0.0)
+        nc.vector.memset(ind[0:D, 0:1], 1.0 / D)
+        nc.vector.memset(ind[D:P, 1:2], 1.0 / D)
         for y, gain in enumerate((q_norm_w, k_norm_w)):
             row = gain.rearrange("(o d) -> o d", o=1)
             nc.scalar.dma_start(out=zrow[y : y + 1, 0:D], in_=row)
@@ -194,19 +199,7 @@ def tile_qwen3nextattentionforengine_pa_t_kernel(
                     start=True,
                     stop=True,
                 )
-            va = ps_a.tile([P, 512], F32, name="va")
-            for t in range(n):
-                nc.tensor.matmul_mx(
-                    out=va[:, t * 256 : (t + 1) * 256],
-                    lhsT=codes[:, t * P : (t + 1) * P].bitcast(FP8X4),
-                    lhsT_scale=scales[:, t * P : (t + 1) * P],
-                    rhs=w_codes[:].bitcast(FP8X4),
-                    rhs_scale=w_scales[:],
-                    start=True,
-                    stop=True,
-                )
             st[("vt", k)] = vt
-            st[("va", k)] = va
 
         def stage_u(k):
             n = UNITS[k]
@@ -219,22 +212,31 @@ def tile_qwen3nextattentionforengine_pa_t_kernel(
                     scale=wcol[:, y : y + 1],
                 )
             st[("ut", k)] = ut
+            sq = sqp.tile([P, n * 256], F32, name="sq")
+            nc.scalar.activation(out=sq[:], in_=st[("vt", k)][:, 0 : n * 256], func=ACT.Square)
+            st[("sq", k)] = sq
 
-        def stage_q(k):
+        def stage_m(k):
             n = UNITS[k]
-            va = st[("va", k)]
-            junk = jkp.tile([P, n * 256], BF16, name="junk")
-            ss = stp.tile([P, n * 4], F32, name="ss")
-            for i in range(n * 4):
-                nc.scalar.activation(
-                    out=junk[:, i * D : (i + 1) * D],
-                    in_=va[:, i * D : (i + 1) * D],
-                    func=ACT.Square,
-                    accum_out=ss[:, i : i + 1],
-                )
+            sq = st[("sq", k)]
+            ssp = ps_s.tile([P, 4 * NIND], F32, name="ssp")
+            for t in range(n):
+                for y in range(2):
+                    c = (t * 2 + y) * NIND
+                    s = (y * n + t) * P
+                    nc.tensor.matmul(
+                        out=ssp[:, c : c + NIND], lhsT=sq[:, s : s + P], rhs=ind[:], start=True, stop=True
+                    )
+            st[("ssp", k)] = ssp
+
+        def stage_r(k):
+            n = UNITS[k]
             rstd = stp.tile([P, n * 4], F32, name="rstd")
             nc.scalar.activation(
-                out=rstd[:], in_=ss[:], func=ACT.Abs_reciprocal_sqrt, scale=1.0 / D, bias=eps_t[:, 0:1]
+                out=rstd[:].rearrange("p (m h) -> p m h", h=2),
+                in_=st[("ssp", k)][:, 0 : 2 * n * NIND].rearrange("p (m h) -> p m h", h=NIND)[:, :, 0:2],
+                func=ACT.Abs_reciprocal_sqrt,
+                bias=eps_t[:, 0:1],
             )
             st[("rstd", k)] = rstd
 
@@ -290,23 +292,26 @@ def tile_qwen3nextattentionforengine_pa_t_kernel(
         def on(k):
             return 0 <= k < NU
 
-        for i in range(NU + 5):
+        for i in range(NU + 6):
             if on(i):
                 load_until(first[i] + AHEAD)
             if on(i - 3):
                 stage_d(i - 3)
-            if on(i - 4):
-                stage_u(i - 4)
-                stage_t(i - 4)
-                stage_q(i - 4)
-            if on(i - 2):
-                stage_c(i - 2)
-            if on(i - 1):
-                stage_b(i - 1)
             if on(i):
                 stage_a(i)
             if on(i - 5):
-                stage_f(i - 5)
-                stage_h(i - 5)
-            if on(i - 3) and first[i - 3] % SWT == 0:
-                stage_cs(first[i - 3] // SWT)
+                stage_t(i - 5)
+                stage_m(i - 5)
+            if on(i - 4):
+                stage_u(i - 4)
+            if on(i - 6):
+                stage_r(i - 6)
+            if on(i - 1):
+                stage_b(i - 1)
+            if on(i - 2):
+                stage_c(i - 2)
+            if on(i - 6):
+                stage_f(i - 6)
+                stage_h(i - 6)
+            if on(i - 4) and first[i - 4] % SWT == 0:
+                stage_cs(first[i - 4] // SWT)

from contextlib import ExitStack

import concourse.mybir as mybir
from concourse.masks import make_identity

F32 = mybir.dt.float32
BF16 = mybir.dt.bfloat16
U32 = mybir.dt.uint32
U8 = mybir.dt.uint8
FP8X4 = mybir.dt.float8_e4m3fn_x4
ALU = mybir.AluOpType
ACT = mybir.ActivationFunctionType

P = 128
HID = 512
D = 64
HALF = 32
NT = 64
UNITS = [1, 1] + [2] * 30 + [1, 1]
XLOADS = [1, 1, 2] + [4] * 15
CST = 16
SWT = 4
AHEAD = 24
EPS = 1e-6
NIND = 48
FLOPS = 2 * 8192 * 512 * 256


def tile_qwen3nextattentionforengine_pa_t_kernel(
    tc, hidden_states, cos, sin, Wq_query, Wk, q_norm_w, k_norm_w, out_0, out_1
):
    nc = tc.nc
    x_v = hidden_states.rearrange("b (s c) k -> (b s) c k", c=NT)
    cos_v = cos.rearrange("b (s c) j -> (b s) c j", c=NT)
    sin_v = sin.rearrange("b (s c) j -> (b s) c j", c=NT)
    out_v = [
        out_0.rearrange("b (s c) h d -> (b s) c (h d)", c=NT),
        out_1.rearrange("b (s c) h d -> (b s) c (h d)", c=NT),
    ]
    first = [sum(UNITS[:k]) for k in range(len(UNITS))]
    NU = len(UNITS)

    with ExitStack() as ctx:
        const = ctx.enter_context(tc.tile_pool(name="const", bufs=1))
        xp = ctx.enter_context(tc.tile_pool(name="xp", bufs=1))
        csp = ctx.enter_context(tc.tile_pool(name="csp", bufs=NT // CST))
        grp = ctx.enter_context(tc.tile_pool(name="grp", bufs=4))
        cdp = ctx.enter_context(tc.tile_pool(name="cdp", bufs=4))
        utp = ctx.enter_context(tc.tile_pool(name="utp", bufs=4))
        sqp = ctx.enter_context(tc.tile_pool(name="sqp", bufs=4))
        stp = ctx.enter_context(tc.tile_pool(name="stp", bufs=4))
        ttp = ctx.enter_context(tc.tile_pool(name="ttp", bufs=4))
        outp = ctx.enter_context(tc.tile_pool(name="outp", bufs=6))
        ps_x = ctx.enter_context(tc.psum_pool(name="ps_x", bufs=2))
        ps_v = ctx.enter_context(tc.psum_pool(name="ps_v", bufs=2))
        ps_s = ctx.enter_context(tc.psum_pool(name="ps_s", bufs=2))
        ps_u = ctx.enter_context(tc.psum_pool(name="ps_u", bufs=2))
        ctx.enter_context(tc.manual_schedule())

        w_sb = const.tile([P, 2 * HID], BF16)
        nc.scalar.dma_start(out=w_sb[:, 0:HID], in_=Wq_query)
        nc.scalar.dma_start(out=w_sb[:, HID : 2 * HID], in_=Wk)

        x_tile = {}
        cs_sb = {}
        sraw_sb = {}

        def load_cs(j):
            c0 = j * CST
            cs = csp.tile([P, 2 * CST * D], BF16, name="cs")
            nc.sync.dma_start(
                out=cs[:, 0 : CST * D].rearrange("p (c j) -> p c j", c=CST),
                in_=cos_v[:, c0 : c0 + CST, :],
            )
            sraw = csp.tile([P, CST * D], BF16, name="sraw")
            nc.sync.dma_start(
                out=sraw[:].rearrange("p (c j) -> p c j", c=CST), in_=sin_v[:, c0 : c0 + CST, :]
            )
            cs_sb[j] = cs
            sraw_sb[j] = sraw

        def load_x(l):
            c0 = sum(XLOADS[:l])
            n = XLOADS[l]
            xg = xp.tile([P, n * HID], BF16, name="x%d" % l)
            nc.sync.dma_start(
                out=xg[:].rearrange("p (c k) -> p c k", c=n), in_=x_v[:, c0 : c0 + n, :]
            )
            for t in range(n):
                x_tile[c0 + t] = (xg, t)
            if l == 3:
                load_cs(0)
            elif l > 3 and c0 % CST == 0:
                load_cs(c0 // CST)

        loaded = [0]

        def load_until(tile):
            while loaded[0] < len(XLOADS) and sum(XLOADS[: loaded[0]]) < tile:
                load_x(loaded[0])
                loaded[0] += 1

        load_until(AHEAD)

        ident = const.tile([P, P], F32)
        make_identity(nc, ident[:])
        ident_b = const.tile([P, P], BF16)
        make_identity(nc, ident_b[:])
        eps_t = const.tile([P, 1], F32)
        nc.vector.memset(eps_t[:], EPS)
        zrow = const.tile([P, P], BF16)
        nc.vector.memset(zrow[:], 0.0)
        ind = const.tile([P, NIND], F32)
        nc.vector.memset(ind[:], 0.0)
        nc.vector.memset(ind[0:D, 0:1], 1.0 / D)
        nc.vector.memset(ind[D:P, 1:2], 1.0 / D)
        for y, gain in enumerate((q_norm_w, k_norm_w)):
            row = gain.rearrange("(o d) -> o d", o=1)
            nc.scalar.dma_start(out=zrow[y : y + 1, 0:D], in_=row)
            nc.scalar.dma_start(out=zrow[y : y + 1, D:P], in_=row)
        warm = const.tile([P, 1], F32)
        nc.scalar.activation(out=warm[:], in_=eps_t[:], func=ACT.Abs_reciprocal_sqrt)

        w_f = w_sb[:].bitcast(F32)
        wt = ps_v.tile([P, 512], F32, name="vt")
        for i in range(4):
            y, u = i // 2, i % 2
            nc.tensor.transpose(
                wt[:, i * P : (i + 1) * P], w_f[:, y * 256 + u : (y + 1) * 256 : 2], ident[:]
            )
        w_gr = const.tile([P, 1024], BF16, align_bytes=64)
        nc.vector.tensor_copy(
            out=w_gr[:].bitcast(F32).rearrange("p (t f u) -> p t f u", t=2, u=2),
            in_=wt[:].rearrange("p (t u f) -> p t f u", t=2, u=2),
        )
        w_codes = const.tile([P, 256], U32, align_bytes=64)
        w_scales = const.tile([P, 256], U8, align_bytes=64)
        nc.vector.quantize_mx(out=w_codes[:].bitcast(FP8X4), scales=w_scales[:], in_=w_gr[:])

        gt_ps = ps_u.tile([P, P], BF16, name="up")
        nc.tensor.transpose(gt_ps[:], zrow[:], ident_b[:])
        wcol = const.tile([P, 2], F32)
        nc.vector.tensor_copy(out=wcol[:], in_=gt_ps[:, 0:2])

        st = {}

        def stage_cs(j):
            c0 = j * SWT % CST
            dst = cs_sb[j * SWT // CST][:, CST * D : 2 * CST * D].rearrange("p (c j) -> p c j", c=CST)
            dst = dst[:, c0 : c0 + SWT, :]
            src = sraw_sb[j * SWT // CST][:].rearrange("p (c j) -> p c j", c=CST)[:, c0 : c0 + SWT, :]
            nc.gpsimd.tensor_scalar(
                out=dst[:, :, 0:HALF], in0=src[:, :, HALF:D], scalar1=1.0, scalar2=0.0,
                op0=ALU.mult, op1=ALU.add,
            )
            nc.gpsimd.tensor_scalar(
                out=dst[:, :, HALF:D], in0=src[:, :, 0:HALF], scalar1=-1.0, scalar2=0.0,
                op0=ALU.mult, op1=ALU.add,
            )

        def stage_a(k):
            xt = ps_x.tile([P, 512], F32, name="xt")
            for i in range(UNITS[k]):
                xg, t = x_tile[first[k] + i]
                x_f = xg[:].bitcast(F32)
                for u in range(2):
                    c = (i * 2 + u) * P
                    nc.tensor.transpose(
                        xt[:, c : c + P], x_f[:, t * 256 + u : (t + 1) * 256 : 2], ident[:]
                    )
            st[("xt", k)] = xt

        def stage_b(k):
            n = UNITS[k]
            gr = grp.tile([P, n * 512], BF16, name="gr", align_bytes=64)
            out = gr[:].bitcast(F32).rearrange("p (t r u) -> p t r u", t=n, u=2)
            src = st[("xt", k)][:, 0 : n * 256].rearrange("p (t u r) -> p t r u", t=n, u=2)
            nc.scalar.copy(out=out, in_=src)
            st[("gr", k)] = gr

        def stage_c(k):
            n = UNITS[k]
            codes = cdp.tile([P, n * P], U32, name="codes", align_bytes=64)
            scales = cdp.tile([P, n * P], U8, name="scales", align_bytes=64)
            nc.vector.quantize_mx(out=codes[:].bitcast(FP8X4), scales=scales[:], in_=st[("gr", k)][:])
            st[("cd", k)] = (codes, scales)

        def stage_d(k):
            n = UNITS[k]
            codes, scales = st[("cd", k)]
            vt = ps_v.tile([P, 512], F32, name="vt")
            for y in range(2):
                nc.tensor.matmul_mx(
                    out=vt[:, y * n * P : (y + 1) * n * P],
                    lhsT=w_codes[:, y * P : (y + 1) * P].bitcast(FP8X4),
                    lhsT_scale=w_scales[:, y * P : (y + 1) * P],
                    rhs=codes[:].bitcast(FP8X4),
                    rhs_scale=scales[:],
                    start=True,
                    stop=True,
                )
            st[("vt", k)] = vt

        def stage_u(k):
            n = UNITS[k]
            ut = utp.tile([P, n * 256], F32, name="ut")
            for y in range(2):
                nc.scalar.activation(
                    out=ut[:, y * n * P : (y + 1) * n * P],
                    in_=st[("vt", k)][:, y * n * P : (y + 1) * n * P],
                    func=ACT.Copy,
                    scale=wcol[:, y : y + 1],
                )
            st[("ut", k)] = ut
            sq = sqp.tile([P, n * 256], F32, name="sq")
            nc.scalar.activation(out=sq[:], in_=st[("vt", k)][:, 0 : n * 256], func=ACT.Square)
            st[("sq", k)] = sq

        def stage_m(k):
            n = UNITS[k]
            sq = st[("sq", k)]
            ssp = ps_s.tile([P, 4 * NIND], F32, name="ssp")
            for t in range(n):
                for y in range(2):
                    c = (t * 2 + y) * NIND
                    s = (y * n + t) * P
                    nc.tensor.matmul(
                        out=ssp[:, c : c + NIND], lhsT=sq[:, s : s + P], rhs=ind[:], start=True, stop=True
                    )
            st[("ssp", k)] = ssp

        def stage_r(k):
            n = UNITS[k]
            rstd = stp.tile([P, n * 4], F32, name="rstd")
            nc.scalar.activation(
                out=rstd[:].rearrange("p (m h) -> p m h", h=2),
                in_=st[("ssp", k)][:, 0 : 2 * n * NIND].rearrange("p (m h) -> p m h", h=NIND)[:, :, 0:2],
                func=ACT.Abs_reciprocal_sqrt,
                bias=eps_t[:, 0:1],
            )
            st[("rstd", k)] = rstd

        def stage_t(k):
            n = UNITS[k]
            up = ps_u.tile([P, 512], F32, name="up")
            ut = st[("ut", k)]
            for t in range(n):
                for y in range(2):
                    c = (t * 2 + y) * P
                    s = (y * n + t) * P
                    nc.tensor.transpose(up[:, c : c + P], ut[:, s : s + P], ident[:])
            st[("up", k)] = up

        def stage_f(k):
            n = UNITS[k]
            rstd = st[("rstd", k)]
            up = st[("up", k)]
            tt = ttp.tile([P, n * 512], F32, name="tt")
            for t in range(n):
                tile = first[k] + t
                csv = cs_sb[tile // CST][:].rearrange("p (r c j) -> p r c j", r=2, c=CST)
                for yh in range(4):
                    si = t * 4 + yh
                    ti = (yh // 2) * 2 * n + t * 2 + yh % 2
                    nc.vector.scalar_tensor_tensor(
                        out=tt[:, ti * 128 : (ti + 1) * 128].rearrange("p (r j) -> p r j", r=2),
                        in0=csv[:, :, tile % CST, :],
                        scalar=rstd[:, si : si + 1],
                        in1=up[:, si * D : (si + 1) * D].unsqueeze(1).to_broadcast([P, 2, D]),
                        op0=ALU.mult,
                        op1=ALU.mult,
                    )
            st[("tt", k)] = tt

        def stage_h(k):
            n = UNITS[k]
            ttv = st[("tt", k)][:].rearrange("p (n r j) -> p n r j", r=2, j=D)
            o = outp.tile([P, n * 256], F32, name="o")
            ov = o[:].rearrange("p (n j) -> p n j", j=D)
            nc.gpsimd.tensor_tensor(
                out=ov.rearrange("p n (a i) -> p n a i", a=2),
                in0=ttv[:, :, 0, :].rearrange("p n (a i) -> p n a i", a=2),
                in1=ttv[:, :, 1, :].rearrange("p n (a i) -> p n a i", a=2)[:, :, ::-1, :],
                op=ALU.add,
            )
            for y in range(2):
                nc.sync.dma_start(
                    out=out_v[y][:, first[k] : first[k] + n, :],
                    in_=o[:, y * n * 128 : (y + 1) * n * 128].rearrange("p (t f) -> p t f", t=n),
                )

        def on(k):
            return 0 <= k < NU

        for i in range(NU + 6):
            if on(i):
                load_until(first[i] + AHEAD)
            if on(i - 3):
                stage_d(i - 3)
            if on(i):
                stage_a(i)
            if on(i - 5):
                stage_t(i - 5)
                stage_m(i - 5)
            if on(i - 4):
                stage_u(i - 4)
            if on(i - 6):
                stage_r(i - 6)
            if on(i - 1):
                stage_b(i - 1)
            if on(i - 2):
                stage_c(i - 2)
            if on(i - 6):
                stage_f(i - 6)
                stage_h(i - 6)
            if on(i - 4) and first[i - 4] % SWT == 0:
                stage_cs(first[i - 4] // SWT)
